import numpy as np
import ml_dtypes


def mxq(x, axis, fmt="e4m3"):
    dtype, down = {"e4m3": (ml_dtypes.float8_e4m3fn, 7), "e5m2": (ml_dtypes.float8_e5m2, 14)}[fmt]
    v = np.moveaxis(np.asarray(x, np.float32).astype(ml_dtypes.bfloat16).astype(np.float64), axis, -1)
    blocks = v.reshape(v.shape[:-1] + (-1, 32))
    amax = np.abs(blocks).max(-1, keepdims=True)
    byte = np.maximum(np.where(amax > 0, np.frexp(amax)[1] - 1 + 127, 0) - down, 1)
    scale = np.exp2(byte - 127.0)
    codes = (blocks / scale).astype(np.float32).astype(dtype).astype(np.float64)
    return np.moveaxis((codes * scale).reshape(v.shape), -1, axis)


WIDE = False


def mx_kscale(k):
    if not WIDE:
        return np.ones(k)
    levels = np.array([10, -10, 5, -5, 0])
    a = np.random.permutation(np.resize(levels, k // 512 * 4)).reshape(k // 512, 4)
    idx = np.arange(k)
    return np.exp2(a[idx // 512, idx % 128 // 32])


BF16 = ml_dtypes.bfloat16


def bf(x):
    return np.asarray(x, np.float32).astype(BF16)


def f64(x):
    return np.asarray(x).astype(np.float64)


B, E, S, H = 1, 512, 512, 4
DH = E // H


def setup_inputs():
    s = mx_kscale(S)
    return {"x_proj": bf(np.random.standard_normal((B, S, E)) * s[None, :, None]),
            "mix_mat": bf(np.random.standard_normal((H, S, S)) * np.sqrt(2.0 / S) / s[None, :, None]),
            "mix_b": bf(np.random.standard_normal((H, S)) * 0.2),
            "out_w": bf(np.random.standard_normal((E, E)) / np.sqrt(E)),
            "out_b": bf(np.random.standard_normal(E) * 0.2)}


def reference(x_proj, mix_mat, mix_b, out_w, out_b):
    p = f64(x_proj).reshape(B, S, H, DH).transpose(0, 2, 3, 1)
    idx = np.arange(S)
    keep = idx[None, :] >= idx[:, None]
    wm = np.where(keep[None], f64(mix_mat), 0.0)
    mixed = (mxq(p, 3, "e4m3") @ mxq(wm, 1, "e4m3")) + f64(mix_b)[None, :, None, :]
    y = mixed.transpose(0, 3, 1, 2).reshape(B, S, E)
    out = (mxq(y, 2, "e4m3") @ mxq(f64(out_w), 1, "e4m3").T) + f64(out_b)
    return out.transpose(0, 2, 1)

@@ -1,0 +1,194 @@
+import concourse.mybir as mybir
+from concourse.masks import make_identity
+
+BF16 = mybir.dt.bfloat16
+F32 = mybir.dt.float32
+U32 = mybir.dt.uint32
+U8 = mybir.dt.uint8
+FP8X4 = mybir.dt.float8_e4m3fn_x4
+ALU = mybir.AluOpType
+ACT = mybir.ActivationFunctionType
+
+P = 128
+PACK = 4
+HEADS = 4
+TOKENS = 512
+CHANNELS = 512
+CHUNK = 128
+N_CHUNKS = TOKENS // CHUNK
+O_TILES = CHANNELS // P
+HEADS_ON_SCALAR = 2
+
+FLOPS = 2 * HEADS * P * TOKENS * TOKENS + 2 * CHANNELS * CHANNELS * TOKENS
+
+
+def tile_mixerblock_pa_s_kernel(tc, x_proj, mix_mat, mix_b, out_w, out_b, out):
+    nc = tc.nc
+    with tc.tile_pool(name="keep", bufs=1) as keep, tc.psum_pool(name="psum", bufs=2) as psum:
+        x_raw = keep.tile([P, PACK, CHANNELS], BF16)
+        x_grouped = keep.tile([P, CHANNELS, PACK], BF16, align_bytes=64)
+        x_codes = keep.tile([P, CHANNELS], U32, align_bytes=64)
+        x_scales = keep.tile([P, CHANNELS], U8, align_bytes=64)
+
+        mix_raw = keep.tile([P, PACK, HEADS, TOKENS], BF16)
+        mix_grouped = keep.tile([P, N_CHUNKS, HEADS, CHUNK, PACK], BF16, align_bytes=64)
+        mix_codes = keep.tile([P, N_CHUNKS, HEADS * CHUNK], U32, align_bytes=64)
+        mix_scales = keep.tile([P, N_CHUNKS, HEADS * CHUNK], U8, align_bytes=64)
+
+        w_rows = keep.tile([P, O_TILES, CHANNELS], BF16)
+        w_grouped = keep.tile([P, O_TILES, P, PACK], BF16, align_bytes=64)
+        w_codes = keep.tile([P, CHANNELS], U32, align_bytes=64)
+        w_scales = keep.tile([P, CHANNELS], U8, align_bytes=64)
+
+        mix_bias = keep.tile([P, HEADS, TOKENS], BF16)
+        out_bias_bf = keep.tile([P, O_TILES], BF16)
+        out_bias = keep.tile([P, O_TILES], F32)
+
+        y_grouped = keep.tile([P, N_CHUNKS, CHUNK, PACK], BF16, align_bytes=64)
+        y_codes = keep.tile([P, N_CHUNKS, CHUNK], U32, align_bytes=64)
+        y_scales = keep.tile([P, N_CHUNKS, CHUNK], U8, align_bytes=64)
+        result = keep.tile([P, O_TILES, TOKENS], F32)
+
+        ident = keep.tile([P, P], BF16)
+        keep_f32 = keep.tile([P, P], F32)
+        keep_mask = keep.tile([P, P], BF16)
+
+        nc.sync.dma_start(out=x_raw[:], in_=x_proj.rearrange("b (j p) c -> p (b j) c", p=P))
+        nc.scalar.dma_start(out=mix_bias[:], in_=mix_b.partition_broadcast(P))
+        with nc.allow_non_contiguous_dma(reason="512 bias values, one to a partition"):
+            nc.scalar.dma_start(out=out_bias_bf[:], in_=out_b.rearrange("(m p) -> p m", p=P))
+
+        def load_mix_plane(j):
+            nc.sync.dma_start(
+                out=mix_raw[:, j, :, j * CHUNK :],
+                in_=mix_mat[:, j * P : (j + 1) * P, j * CHUNK :].rearrange("h p s -> p h s"),
+            )
+
+        load_mix_plane(0)
+        nc.sync.dma_start(out=w_rows[:], in_=out_w.rearrange("(m p) c -> p m c", p=P))
+        for j in range(1, PACK):
+            load_mix_plane(j)
+
+        make_identity(nc, ident[:])
+        nc.gpsimd.memset(keep_f32[:], 1.0)
+        nc.gpsimd.affine_select(
+            out=keep_f32[:],
+            in_=keep_f32[:],
+            pattern=[[1, P]],
+            compare_op=ALU.is_ge,
+            fill=0.0,
+            base=0,
+            channel_multiplier=-1,
+        )
+        nc.vector.tensor_copy(out=keep_mask[:], in_=keep_f32[:])
+        for j in range(1, PACK):
+            nc.vector.memset(mix_raw[:, j, :, : j * CHUNK], 0.0)
+        nc.vector.tensor_copy(out=out_bias[:], in_=out_bias_bf[:])
+
+        nc.vector.tensor_copy(out=x_grouped[:], in_=x_raw[:].rearrange("p j c -> p c j"))
+        nc.vector.quantize_mx(
+            out=x_codes[:].bitcast(FP8X4),
+            scales=x_scales[:],
+            in_=x_grouped[:].rearrange("p c j -> p (c j)"),
+        )
+
+        def quantise_mix_chunk(i):
+            cols = slice(i * CHUNK, (i + 1) * CHUNK)
+            nc.vector.tensor_tensor(
+                out=mix_raw[:, i, :, cols],
+                in0=mix_raw[:, i, :, cols],
+                in1=keep_mask[:].unsqueeze(1).to_broadcast([P, HEADS, CHUNK]),
+                op=ALU.mult,
+            )
+            split = HEADS - HEADS_ON_SCALAR
+            nc.vector.tensor_copy(
+                out=mix_grouped[:, i, :split],
+                in_=mix_raw[:, :, :split, cols].rearrange("p j h s -> p h s j"),
+            )
+            nc.scalar.copy(
+                out=mix_grouped[:, i, split:],
+                in_=mix_raw[:, :, split:, cols].rearrange("p j h s -> p h s j"),
+            )
+            nc.vector.quantize_mx(
+                out=mix_codes[:, i, :].bitcast(FP8X4),
+                scales=mix_scales[:, i, :],
+                in_=mix_grouped[:, i].rearrange("p h s j -> p (h s j)"),
+            )
+
+        def quantise_out_w():
+            for half in range(O_TILES // 2):
+                w_t = psum.tile([P, 2, PACK, P], BF16)
+                for k in range(2):
+                    m = 2 * half + k
+                    for t in range(PACK):
+                        nc.tensor.transpose(w_t[:, k, t, :], w_rows[:, m, t * P : (t + 1) * P], ident[:])
+                for k in range(2):
+                    nc.scalar.copy(
+                        out=w_grouped[:, 2 * half + k],
+                        in_=w_t[:, k].rearrange("p t o -> p o t"),
+                    )
+            nc.vector.quantize_mx(
+                out=w_codes[:].bitcast(FP8X4),
+                scales=w_scales[:],
+                in_=w_grouped[:].rearrange("p m o t -> p (m o t)"),
+            )
+
+        def mix_tokens(i):
+            cols = slice(i * CHUNK, (i + 1) * CHUNK)
+            mixed = psum.tile([P, HEADS, CHUNK], F32)
+            for h in range(HEADS):
+                head = slice(h * P, (h + 1) * P)
+                nc.tensor.matmul_mx(
+                    out=mixed[:, h, :],
+                    lhsT=x_codes[:, head].bitcast(FP8X4),
+                    lhsT_scale=x_scales[:, head],
+                    rhs=mix_codes[:, i, head].bitcast(FP8X4),
+                    rhs_scale=mix_scales[:, i, head],
+                    start=True,
+                    stop=True,
+                )
+            nc.vector.tensor_tensor(
+                out=y_grouped[:, i],
+                in0=mixed[:].rearrange("p h s -> p s h"),
+                in1=mix_bias[:, :, cols].rearrange("p h s -> p s h"),
+                op=ALU.add,
+            )
+            nc.vector.quantize_mx(
+                out=y_codes[:, i, :].bitcast(FP8X4),
+                scales=y_scales[:, i, :],
+                in_=y_grouped[:, i].rearrange("p s h -> p (s h)"),
+            )
+
+        def project(i):
+            cols = slice(i * CHUNK, (i + 1) * CHUNK)
+            projected = psum.tile([P, O_TILES, CHUNK], F32)
+            for m in range(O_TILES):
+                rows = slice(m * P, (m + 1) * P)
+                nc.tensor.matmul_mx(
+                    out=projected[:, m, :],
+                    lhsT=w_codes[:, rows].bitcast(FP8X4),
+                    lhsT_scale=w_scales[:, rows],
+                    rhs=y_codes[:, i, :].bitcast(FP8X4),
+                    rhs_scale=y_scales[:, i, :],
+                    start=True,
+                    stop=True,
+                )
+            for m in range(O_TILES):
+                nc.scalar.activation(
+                    out=result[:, m, cols],
+                    in_=projected[:, m, :],
+                    func=ACT.Identity,
+                    bias=out_bias[:, m : m + 1],
+                )
+            nc.sync.dma_start(
+                out=out.rearrange("b (m p) s -> p (b m) s", p=P)[:, :, cols],
+                in_=result[:, :, cols],
+            )
+
+        quantise_mix_chunk(0)
+        quantise_out_w()
+        for i in range(N_CHUNKS):
+            if i + 1 < N_CHUNKS:
+                quantise_mix_chunk(i + 1)
+            mix_tokens(i)
+            project(i)

@@ -17,6 +17,7 @@ CHANNELS = 512
 CHUNK = 128
 N_CHUNKS = TOKENS // CHUNK
 O_TILES = CHANNELS // P
+BIAS_ROWS_MIX = HEADS * N_CHUNKS
 HEADS_ON_SCALAR = 2
 
 FLOPS = 2 * HEADS * P * TOKENS * TOKENS + 2 * CHANNELS * CHANNELS * TOKENS
@@ -24,7 +25,9 @@ FLOPS = 2 * HEADS * P * TOKENS * TOKENS + 2 * CHANNELS * CHANNELS * TOKENS
 
 def tile_mixerblock_pa_s_kernel(tc, x_proj, mix_mat, mix_b, out_w, out_b, out):
     nc = tc.nc
-    with tc.tile_pool(name="keep", bufs=1) as keep, tc.psum_pool(name="psum", bufs=2) as psum:
+    with tc.tile_pool(name="keep", bufs=1) as keep, tc.psum_pool(name="psum", bufs=3) as psum, tc.psum_pool(
+        name="setup", bufs=2
+    ) as setup:
         x_raw = keep.tile([P, PACK, CHANNELS], BF16)
         x_grouped = keep.tile([P, CHANNELS, PACK], BF16, align_bytes=64)
         x_codes = keep.tile([P, CHANNELS], U32, align_bytes=64)
@@ -40,8 +43,9 @@ def tile_mixerblock_pa_s_kernel(tc, x_proj, mix_mat, mix_b, out_w, out_b, out):
         w_codes = keep.tile([P, CHANNELS], U32, align_bytes=64)
         w_scales = keep.tile([P, CHANNELS], U8, align_bytes=64)
 
-        mix_bias = keep.tile([P, HEADS, TOKENS], BF16)
-        out_bias_bf = keep.tile([P, O_TILES], BF16)
+        bias_rows = keep.tile([P, P], BF16)
+        mix_bias_cols = keep.tile([P, BIAS_ROWS_MIX], BF16)
+        mix_bias = keep.tile([P, BIAS_ROWS_MIX, CHUNK], BF16)
         out_bias = keep.tile([P, O_TILES], F32)
 
         y_grouped = keep.tile([P, N_CHUNKS, CHUNK, PACK], BF16, align_bytes=64)
@@ -54,9 +58,11 @@ def tile_mixerblock_pa_s_kernel(tc, x_proj, mix_mat, mix_b, out_w, out_b, out):
         keep_mask = keep.tile([P, P], BF16)
 
         nc.sync.dma_start(out=x_raw[:], in_=x_proj.rearrange("b (j p) c -> p (b j) c", p=P))
-        nc.scalar.dma_start(out=mix_bias[:], in_=mix_b.partition_broadcast(P))
-        with nc.allow_non_contiguous_dma(reason="512 bias values, one to a partition"):
-            nc.scalar.dma_start(out=out_bias_bf[:], in_=out_b.rearrange("(m p) -> p m", p=P))
+        nc.vector.memset(bias_rows[:], 0.0)
+        nc.scalar.dma_start(out=bias_rows[:BIAS_ROWS_MIX, :], in_=mix_b.rearrange("h (i s) -> (h i) s", s=CHUNK))
+        nc.scalar.dma_start(
+            out=bias_rows[BIAS_ROWS_MIX : BIAS_ROWS_MIX + O_TILES, :], in_=out_b.rearrange("(m p) -> m p", p=P)
+        )
 
         def load_mix_plane(j):
             nc.sync.dma_start(
@@ -83,7 +89,17 @@ def tile_mixerblock_pa_s_kernel(tc, x_proj, mix_mat, mix_b, out_w, out_b, out):
         nc.vector.tensor_copy(out=keep_mask[:], in_=keep_f32[:])
         for j in range(1, PACK):
             nc.vector.memset(mix_raw[:, j, :, : j * CHUNK], 0.0)
-        nc.vector.tensor_copy(out=out_bias[:], in_=out_bias_bf[:])
+
+        bias_cols = setup.tile([P, P], BF16, tag="setup")
+        nc.tensor.transpose(bias_cols[:], bias_rows[:], ident[:])
+        nc.vector.tensor_copy(out=mix_bias_cols[:], in_=bias_cols[:, :BIAS_ROWS_MIX])
+        nc.vector.tensor_copy(out=out_bias[:], in_=bias_cols[:, BIAS_ROWS_MIX : BIAS_ROWS_MIX + O_TILES])
+        for half in range(2):
+            spread = setup.tile([P, BIAS_ROWS_MIX // 2, CHUNK], BF16, tag="setup")
+            for k in range(BIAS_ROWS_MIX // 2):
+                r = half * (BIAS_ROWS_MIX // 2) + k
+                nc.tensor.transpose(spread[:, k, :], mix_bias_cols[:, r : r + 1].to_broadcast([P, P]), ident[:])
+            nc.scalar.copy(out=mix_bias[:, half * (BIAS_ROWS_MIX // 2) : (half + 1) * (BIAS_ROWS_MIX // 2), :], in_=spread[:])
 
         nc.vector.tensor_copy(out=x_grouped[:], in_=x_raw[:].rearrange("p j c -> p c j"))
         nc.vector.quantize_mx(
@@ -117,7 +133,7 @@ def tile_mixerblock_pa_s_kernel(tc, x_proj, mix_mat, mix_b, out_w, out_b, out):
 
         def quantise_out_w():
             for half in range(O_TILES // 2):
-                w_t = psum.tile([P, 2, PACK, P], BF16)
+                w_t = setup.tile([P, 2, PACK, P], BF16, tag="setup")
                 for k in range(2):
                     m = 2 * half + k
                     for t in range(PACK):
@@ -134,7 +150,6 @@ def tile_mixerblock_pa_s_kernel(tc, x_proj, mix_mat, mix_b, out_w, out_b, out):
             )
 
         def mix_tokens(i):
-            cols = slice(i * CHUNK, (i + 1) * CHUNK)
             mixed = psum.tile([P, HEADS, CHUNK], F32)
             for h in range(HEADS):
                 head = slice(h * P, (h + 1) * P)
@@ -150,7 +165,7 @@ def tile_mixerblock_pa_s_kernel(tc, x_proj, mix_mat, mix_b, out_w, out_b, out):
             nc.vector.tensor_tensor(
                 out=y_grouped[:, i],
                 in0=mixed[:].rearrange("p h s -> p s h"),
-                in1=mix_bias[:, :, cols].rearrange("p h s -> p s h"),
+                in1=mix_bias[:].rearrange("p (h i) s -> p i s h", i=N_CHUNKS)[:, i],
                 op=ALU.add,
             )
             nc.vector.quantize_mx(

@@ -17,52 +17,49 @@ CHANNELS = 512
 CHUNK = 128
 N_CHUNKS = TOKENS // CHUNK
 O_TILES = CHANNELS // P
-BIAS_ROWS_MIX = HEADS * N_CHUNKS
-HEADS_ON_SCALAR = 2
+X_HEADS_ON_SCALAR = 1
+MIX_HEADS_ON_SCALAR = 2
 
 FLOPS = 2 * HEADS * P * TOKENS * TOKENS + 2 * CHANNELS * CHANNELS * TOKENS
 
 
 def tile_mixerblock_pa_s_kernel(tc, x_proj, mix_mat, mix_b, out_w, out_b, out):
     nc = tc.nc
-    with tc.tile_pool(name="keep", bufs=1) as keep, tc.psum_pool(name="psum", bufs=3) as psum, tc.psum_pool(
-        name="setup", bufs=2
-    ) as setup:
-        x_raw = keep.tile([P, PACK, CHANNELS], BF16)
-        x_grouped = keep.tile([P, CHANNELS, PACK], BF16, align_bytes=64)
-        x_codes = keep.tile([P, CHANNELS], U32, align_bytes=64)
-        x_scales = keep.tile([P, CHANNELS], U8, align_bytes=64)
+    with tc.tile_pool(name="resident", bufs=1) as resident, tc.psum_pool(name="banks", bufs=3) as banks, tc.psum_pool(
+        name="w_banks", bufs=2
+    ) as w_banks, tc.manual_schedule():
+        x_raw = resident.tile([P, PACK, CHANNELS], BF16)
+        x_grouped = resident.tile([P, CHANNELS, PACK], BF16, align_bytes=64)
+        x_codes = resident.tile([P, CHANNELS], U32, align_bytes=64)
+        x_scales = resident.tile([P, CHANNELS], U8, align_bytes=64)
 
-        mix_raw = keep.tile([P, PACK, HEADS, TOKENS], BF16)
-        mix_grouped = keep.tile([P, N_CHUNKS, HEADS, CHUNK, PACK], BF16, align_bytes=64)
-        mix_codes = keep.tile([P, N_CHUNKS, HEADS * CHUNK], U32, align_bytes=64)
-        mix_scales = keep.tile([P, N_CHUNKS, HEADS * CHUNK], U8, align_bytes=64)
+        mix_raw = resident.tile([P, PACK, HEADS, TOKENS], BF16)
+        mix_grouped = resident.tile([P, N_CHUNKS, HEADS, CHUNK, PACK], BF16, align_bytes=64)
+        mix_codes = resident.tile([P, N_CHUNKS, HEADS * CHUNK], U32, align_bytes=64)
+        mix_scales = resident.tile([P, N_CHUNKS, HEADS * CHUNK], U8, align_bytes=64)
 
-        w_rows = keep.tile([P, O_TILES, CHANNELS], BF16)
-        w_grouped = keep.tile([P, O_TILES, P, PACK], BF16, align_bytes=64)
-        w_codes = keep.tile([P, CHANNELS], U32, align_bytes=64)
-        w_scales = keep.tile([P, CHANNELS], U8, align_bytes=64)
+        w_rows = resident.tile([P, O_TILES, CHANNELS], BF16)
+        w_grouped = resident.tile([P, O_TILES, P, PACK], BF16, align_bytes=64)
+        w_codes = resident.tile([P, CHANNELS], U32, align_bytes=64)
+        w_scales = resident.tile([P, CHANNELS], U8, align_bytes=64)
 
-        bias_rows = keep.tile([P, P], BF16)
-        mix_bias_cols = keep.tile([P, BIAS_ROWS_MIX], BF16)
-        mix_bias = keep.tile([P, BIAS_ROWS_MIX, CHUNK], BF16)
-        out_bias = keep.tile([P, O_TILES], F32)
+        mix_bias = resident.tile([P, HEADS, TOKENS], BF16)
+        out_bias = resident.tile([P, O_TILES], BF16)
 
-        y_grouped = keep.tile([P, N_CHUNKS, CHUNK, PACK], BF16, align_bytes=64)
-        y_codes = keep.tile([P, N_CHUNKS, CHUNK], U32, align_bytes=64)
-        y_scales = keep.tile([P, N_CHUNKS, CHUNK], U8, align_bytes=64)
-        result = keep.tile([P, O_TILES, TOKENS], F32)
+        y_grouped = resident.tile([P, N_CHUNKS, CHUNK, PACK], BF16, align_bytes=64)
+        y_codes = resident.tile([P, N_CHUNKS, CHUNK], U32, align_bytes=64)
+        y_scales = resident.tile([P, N_CHUNKS, CHUNK], U8, align_bytes=64)
+        result = resident.tile([P, O_TILES, TOKENS], F32)
 
-        ident = keep.tile([P, P], BF16)
-        keep_f32 = keep.tile([P, P], F32)
-        keep_mask = keep.tile([P, P], BF16)
+        ident = resident.tile([P, P], BF16)
+        causal_f32 = resident.tile([P, P], F32)
+        causal = resident.tile([P, P], BF16)
 
-        nc.sync.dma_start(out=x_raw[:], in_=x_proj.rearrange("b (j p) c -> p (b j) c", p=P))
-        nc.vector.memset(bias_rows[:], 0.0)
-        nc.scalar.dma_start(out=bias_rows[:BIAS_ROWS_MIX, :], in_=mix_b.rearrange("h (i s) -> (h i) s", s=CHUNK))
-        nc.scalar.dma_start(
-            out=bias_rows[BIAS_ROWS_MIX : BIAS_ROWS_MIX + O_TILES, :], in_=out_b.rearrange("(m p) -> m p", p=P)
-        )
+        mixed_banks = {}
+        projected_banks = {}
+
+        def chunk_cols(i):
+            return slice(i * CHUNK, (i + 1) * CHUNK)
 
         def load_mix_plane(j):
             nc.sync.dma_start(
@@ -70,87 +67,72 @@ def tile_mixerblock_pa_s_kernel(tc, x_proj, mix_mat, mix_b, out_w, out_b, out):
                 in_=mix_mat[:, j * P : (j + 1) * P, j * CHUNK :].rearrange("h p s -> p h s"),
             )
 
+        nc.sync.dma_start(out=x_raw[:], in_=x_proj.rearrange("b (j p) c -> p (b j) c", p=P))
         load_mix_plane(0)
+        load_mix_plane(1)
+        nc.sync.dma_start(out=mix_bias[:], in_=mix_b.partition_broadcast(P))
         nc.sync.dma_start(out=w_rows[:], in_=out_w.rearrange("(m p) c -> p m c", p=P))
-        for j in range(1, PACK):
-            load_mix_plane(j)
+        load_mix_plane(2)
+        load_mix_plane(3)
+        with nc.allow_non_contiguous_dma(reason="512 bias values, one to a partition"):
+            nc.scalar.dma_start(out=out_bias[:], in_=out_b.rearrange("(m p) -> p m", p=P))
 
         make_identity(nc, ident[:])
-        nc.gpsimd.memset(keep_f32[:], 1.0)
+        nc.gpsimd.memset(causal_f32[:], 1.0)
         nc.gpsimd.affine_select(
-            out=keep_f32[:],
-            in_=keep_f32[:],
+            out=causal_f32[:],
+            in_=causal_f32[:],
             pattern=[[1, P]],
             compare_op=ALU.is_ge,
             fill=0.0,
             base=0,
             channel_multiplier=-1,
         )
-        nc.vector.tensor_copy(out=keep_mask[:], in_=keep_f32[:])
         for j in range(1, PACK):
             nc.vector.memset(mix_raw[:, j, :, : j * CHUNK], 0.0)
+        nc.vector.tensor_copy(out=causal[:], in_=causal_f32[:])
 
-        bias_cols = setup.tile([P, P], BF16, tag="setup")
-        nc.tensor.transpose(bias_cols[:], bias_rows[:], ident[:])
-        nc.vector.tensor_copy(out=mix_bias_cols[:], in_=bias_cols[:, :BIAS_ROWS_MIX])
-        nc.vector.tensor_copy(out=out_bias[:], in_=bias_cols[:, BIAS_ROWS_MIX : BIAS_ROWS_MIX + O_TILES])
-        for half in range(2):
-            spread = setup.tile([P, BIAS_ROWS_MIX // 2, CHUNK], BF16, tag="setup")
-            for k in range(BIAS_ROWS_MIX // 2):
-                r = half * (BIAS_ROWS_MIX // 2) + k
-                nc.tensor.transpose(spread[:, k, :], mix_bias_cols[:, r : r + 1].to_broadcast([P, P]), ident[:])
-            nc.scalar.copy(out=mix_bias[:, half * (BIAS_ROWS_MIX // 2) : (half + 1) * (BIAS_ROWS_MIX // 2), :], in_=spread[:])
+        def regroup_x():
+            split = (HEADS - X_HEADS_ON_SCALAR) * P
+            nc.vector.tensor_copy(out=x_grouped[:, :split, :], in_=x_raw[:, :, :split].rearrange("p j c -> p c j"))
+            nc.scalar.copy(out=x_grouped[:, split:, :], in_=x_raw[:, :, split:].rearrange("p j c -> p c j"))
 
-        nc.vector.tensor_copy(out=x_grouped[:], in_=x_raw[:].rearrange("p j c -> p c j"))
-        nc.vector.quantize_mx(
-            out=x_codes[:].bitcast(FP8X4),
-            scales=x_scales[:],
-            in_=x_grouped[:].rearrange("p c j -> p (c j)"),
-        )
+        def quantise_x():
+            nc.vector.quantize_mx(
+                out=x_codes[:].bitcast(FP8X4),
+                scales=x_scales[:],
+                in_=x_grouped[:].rearrange("p c j -> p (c j)"),
+            )
 
-        def quantise_mix_chunk(i):
-            cols = slice(i * CHUNK, (i + 1) * CHUNK)
+        def mask_diagonal(i):
             nc.vector.tensor_tensor(
-                out=mix_raw[:, i, :, cols],
-                in0=mix_raw[:, i, :, cols],
-                in1=keep_mask[:].unsqueeze(1).to_broadcast([P, HEADS, CHUNK]),
+                out=mix_raw[:, i, :, chunk_cols(i)],
+                in0=mix_raw[:, i, :, chunk_cols(i)],
+                in1=causal[:].unsqueeze(1).to_broadcast([P, HEADS, CHUNK]),
                 op=ALU.mult,
             )
-            split = HEADS - HEADS_ON_SCALAR
+
+        def regroup_mix(i):
+            split = HEADS - MIX_HEADS_ON_SCALAR
             nc.vector.tensor_copy(
                 out=mix_grouped[:, i, :split],
-                in_=mix_raw[:, :, :split, cols].rearrange("p j h s -> p h s j"),
+                in_=mix_raw[:, :, :split, chunk_cols(i)].rearrange("p j h s -> p h s j"),
             )
             nc.scalar.copy(
                 out=mix_grouped[:, i, split:],
-                in_=mix_raw[:, :, split:, cols].rearrange("p j h s -> p h s j"),
+                in_=mix_raw[:, :, split:, chunk_cols(i)].rearrange("p j h s -> p h s j"),
             )
+
+        def quantise_mix(i):
             nc.vector.quantize_mx(
                 out=mix_codes[:, i, :].bitcast(FP8X4),
                 scales=mix_scales[:, i, :],
                 in_=mix_grouped[:, i].rearrange("p h s j -> p (h s j)"),
             )
 
-        def quantise_out_w():
-            for half in range(O_TILES // 2):
-                w_t = setup.tile([P, 2, PACK, P], BF16, tag="setup")
-                for k in range(2):
-                    m = 2 * half + k
-                    for t in range(PACK):
-                        nc.tensor.transpose(w_t[:, k, t, :], w_rows[:, m, t * P : (t + 1) * P], ident[:])
-                for k in range(2):
-                    nc.scalar.copy(
-                        out=w_grouped[:, 2 * half + k],
-                        in_=w_t[:, k].rearrange("p t o -> p o t"),
-                    )
-            nc.vector.quantize_mx(
-                out=w_codes[:].bitcast(FP8X4),
-                scales=w_scales[:],
-                in_=w_grouped[:].rearrange("p m o t -> p (m o t)"),
-            )
-
         def mix_tokens(i):
-            mixed = psum.tile([P, HEADS, CHUNK], F32)
+            mixed = banks.tile([P, HEADS, CHUNK], F32)
+            mixed_banks[i] = mixed
             for h in range(HEADS):
                 head = slice(h * P, (h + 1) * P)
                 nc.tensor.matmul_mx(
@@ -162,21 +144,41 @@ def tile_mixerblock_pa_s_kernel(tc, x_proj, mix_mat, mix_b, out_w, out_b, out):
                     start=True,
                     stop=True,
                 )
+
+        def add_mix_bias(i):
             nc.vector.tensor_tensor(
                 out=y_grouped[:, i],
-                in0=mixed[:].rearrange("p h s -> p s h"),
-                in1=mix_bias[:].rearrange("p (h i) s -> p i s h", i=N_CHUNKS)[:, i],
+                in0=mixed_banks[i][:].rearrange("p h s -> p s h"),
+                in1=mix_bias[:, :, chunk_cols(i)].rearrange("p h s -> p s h"),
                 op=ALU.add,
             )
+
+        def quantise_mixed(i):
             nc.vector.quantize_mx(
                 out=y_codes[:, i, :].bitcast(FP8X4),
                 scales=y_scales[:, i, :],
                 in_=y_grouped[:, i].rearrange("p s h -> p (s h)"),
             )
 
+        def transpose_out_w():
+            for half in range(O_TILES // 2):
+                w_t = w_banks.tile([P, 2, PACK, P], BF16)
+                for k in range(2):
+                    for t in range(PACK):
+                        nc.tensor.transpose(w_t[:, k, t, :], w_rows[:, 2 * half + k, t * P : (t + 1) * P], ident[:])
+                for k in range(2):
+                    nc.scalar.copy(out=w_grouped[:, 2 * half + k], in_=w_t[:, k].rearrange("p t o -> p o t"))
+
+        def quantise_out_w():
+            nc.vector.quantize_mx(
+                out=w_codes[:].bitcast(FP8X4),
+                scales=w_scales[:],
+                in_=w_grouped[:].rearrange("p m o t -> p (m o t)"),
+            )
+
         def project(i):
-            cols = slice(i * CHUNK, (i + 1) * CHUNK)
-            projected = psum.tile([P, O_TILES, CHUNK], F32)
+            projected = banks.tile([P, O_TILES, CHUNK], F32)
+            projected_banks[i] = projected
             for m in range(O_TILES):
                 rows = slice(m * P, (m + 1) * P)
                 nc.tensor.matmul_mx(
@@ -188,22 +190,41 @@ def tile_mixerblock_pa_s_kernel(tc, x_proj, mix_mat, mix_b, out_w, out_b, out):
                     start=True,
                     stop=True,
                 )
+
+        def finish(i):
             for m in range(O_TILES):
                 nc.scalar.activation(
-                    out=result[:, m, cols],
-                    in_=projected[:, m, :],
+                    out=result[:, m, chunk_cols(i)],
+                    in_=projected_banks[i][:, m, :],
                     func=ACT.Identity,
                     bias=out_bias[:, m : m + 1],
                 )
             nc.sync.dma_start(
-                out=out.rearrange("b (m p) s -> p (b m) s", p=P)[:, :, cols],
-                in_=result[:, :, cols],
+                out=out.rearrange("b (m p) s -> p (b m) s", p=P)[:, :, chunk_cols(i)],
+                in_=result[:, :, chunk_cols(i)],
             )
 
-        quantise_mix_chunk(0)
-        quantise_out_w()
-        for i in range(N_CHUNKS):
-            if i + 1 < N_CHUNKS:
-                quantise_mix_chunk(i + 1)
-            mix_tokens(i)
-            project(i)
+        regroup_x()
+        mask_diagonal(0)
+        quantise_x()
+        regroup_mix(0)
+        mask_diagonal(1)
+        for step in range(N_CHUNKS + 2):
+            if step < N_CHUNKS:
+                quantise_mix(step)
+                mix_tokens(step)
+            if step + 1 < N_CHUNKS:
+                regroup_mix(step + 1)
+            if step == 0:
+                transpose_out_w()
+            if step >= 2:
+                finish(step - 2)
+            if 1 <= step <= N_CHUNKS:
+                add_mix_bias(step - 1)
+            if step == 1:
+                quantise_out_w()
+            if step + 2 < N_CHUNKS:
+                mask_diagonal(step + 2)
+            if 1 <= step <= N_CHUNKS:
+                quantise_mixed(step - 1)
+                project(step - 1)

@@ -43,8 +43,10 @@ def tile_mixerblock_pa_s_kernel(tc, x_proj, mix_mat, mix_b, out_w, out_b, out):
         w_codes = resident.tile([P, CHANNELS], U32, align_bytes=64)
         w_scales = resident.tile([P, CHANNELS], U8, align_bytes=64)
 
-        mix_bias = resident.tile([P, HEADS, TOKENS], BF16)
-        out_bias = resident.tile([P, O_TILES], BF16)
+        bias_rows = resident.tile([P, P], BF16)
+        mix_bias_cols = resident.tile([P, HEADS * N_CHUNKS], BF16)
+        mix_bias = resident.tile([P, N_CHUNKS, HEADS, CHUNK], BF16)
+        out_bias = resident.tile([P, O_TILES], F32)
 
         y_grouped = resident.tile([P, N_CHUNKS, CHUNK, PACK], BF16, align_bytes=64)
         y_codes = resident.tile([P, N_CHUNKS, CHUNK], U32, align_bytes=64)
@@ -67,15 +69,17 @@ def tile_mixerblock_pa_s_kernel(tc, x_proj, mix_mat, mix_b, out_w, out_b, out):
                 in_=mix_mat[:, j * P : (j + 1) * P, j * CHUNK :].rearrange("h p s -> p h s"),
             )
 
+        nc.vector.memset(bias_rows[:], 0.0)
+        nc.scalar.dma_start(out=bias_rows[: HEADS * N_CHUNKS, :], in_=mix_b.rearrange("h (i s) -> (h i) s", s=CHUNK))
+        nc.scalar.dma_start(
+            out=bias_rows[HEADS * N_CHUNKS : HEADS * N_CHUNKS + O_TILES, :], in_=out_b.rearrange("(m p) -> m p", p=P)
+        )
         nc.sync.dma_start(out=x_raw[:], in_=x_proj.rearrange("b (j p) c -> p (b j) c", p=P))
         load_mix_plane(0)
         load_mix_plane(1)
-        nc.sync.dma_start(out=mix_bias[:], in_=mix_b.partition_broadcast(P))
         nc.sync.dma_start(out=w_rows[:], in_=out_w.rearrange("(m p) c -> p m c", p=P))
         load_mix_plane(2)
         load_mix_plane(3)
-        with nc.allow_non_contiguous_dma(reason="512 bias values, one to a partition"):
-            nc.scalar.dma_start(out=out_bias[:], in_=out_b.rearrange("(m p) -> p m", p=P))
 
         make_identity(nc, ident[:])
         nc.gpsimd.memset(causal_f32[:], 1.0)
@@ -103,6 +107,23 @@ def tile_mixerblock_pa_s_kernel(tc, x_proj, mix_mat, mix_b, out_w, out_b, out):
                 scales=x_scales[:],
                 in_=x_grouped[:].rearrange("p c j -> p (c j)"),
             )
+
+        def stand_biases_up():
+            bias_cols = w_banks.tile([P, P], BF16, tag="w_t")
+            nc.tensor.transpose(bias_cols[:], bias_rows[:], ident[:])
+            nc.vector.tensor_copy(out=mix_bias_cols[:], in_=bias_cols[:, : HEADS * N_CHUNKS])
+            nc.vector.tensor_copy(out=out_bias[:], in_=bias_cols[:, HEADS * N_CHUNKS : HEADS * N_CHUNKS + O_TILES])
+
+        def spread_mix_bias():
+            for half in range(N_CHUNKS // 2):
+                spread = w_banks.tile([P, 2, HEADS, CHUNK], BF16, tag="w_t")
+                for k in range(2):
+                    for h in range(HEADS):
+                        r = h * N_CHUNKS + 2 * half + k
+                        nc.tensor.transpose(
+                            spread[:, k, h, :], mix_bias_cols[:, r : r + 1].to_broadcast([P, P]), ident[:]
+                        )
+                nc.scalar.copy(out=mix_bias[:, 2 * half : 2 * half + 2], in_=spread[:])
 
         def mask_diagonal(i):
             nc.vector.tensor_tensor(
@@ -149,7 +170,7 @@ def tile_mixerblock_pa_s_kernel(tc, x_proj, mix_mat, mix_b, out_w, out_b, out):
             nc.vector.tensor_tensor(
                 out=y_grouped[:, i],
                 in0=mixed_banks[i][:].rearrange("p h s -> p s h"),
-                in1=mix_bias[:, :, chunk_cols(i)].rearrange("p h s -> p s h"),
+                in1=mix_bias[:, i].rearrange("p h s -> p s h"),
                 op=ALU.add,
             )
 
@@ -162,7 +183,7 @@ def tile_mixerblock_pa_s_kernel(tc, x_proj, mix_mat, mix_b, out_w, out_b, out):
 
         def transpose_out_w():
             for half in range(O_TILES // 2):
-                w_t = w_banks.tile([P, 2, PACK, P], BF16)
+                w_t = w_banks.tile([P, 2, PACK, P], BF16, tag="w_t")
                 for k in range(2):
                     for t in range(PACK):
                         nc.tensor.transpose(w_t[:, k, t, :], w_rows[:, 2 * half + k, t * P : (t + 1) * P], ident[:])
@@ -205,9 +226,11 @@ def tile_mixerblock_pa_s_kernel(tc, x_proj, mix_mat, mix_b, out_w, out_b, out):
             )
 
         regroup_x()
+        stand_biases_up()
         mask_diagonal(0)
         quantise_x()
         regroup_mix(0)
+        spread_mix_bias()
         mask_diagonal(1)
         for step in range(N_CHUNKS + 2):
             if step < N_CHUNKS:

@@ -17,7 +17,6 @@ CHANNELS = 512
 CHUNK = 128
 N_CHUNKS = TOKENS // CHUNK
 O_TILES = CHANNELS // P
-X_HEADS_ON_SCALAR = 1
 MIX_HEADS_ON_SCALAR = 2
 
 FLOPS = 2 * HEADS * P * TOKENS * TOKENS + 2 * CHANNELS * CHANNELS * TOKENS
@@ -25,9 +24,7 @@ FLOPS = 2 * HEADS * P * TOKENS * TOKENS + 2 * CHANNELS * CHANNELS * TOKENS
 
 def tile_mixerblock_pa_s_kernel(tc, x_proj, mix_mat, mix_b, out_w, out_b, out):
     nc = tc.nc
-    with tc.tile_pool(name="resident", bufs=1) as resident, tc.psum_pool(name="banks", bufs=3) as banks, tc.psum_pool(
-        name="w_banks", bufs=2
-    ) as w_banks, tc.manual_schedule():
+    with tc.tile_pool(name="resident", bufs=1) as resident, tc.psum_pool(name="banks", bufs=2) as banks, tc.manual_schedule():
         x_raw = resident.tile([P, PACK, CHANNELS], BF16)
         x_grouped = resident.tile([P, CHANNELS, PACK], BF16, align_bytes=64)
         x_codes = resident.tile([P, CHANNELS], U32, align_bytes=64)
@@ -69,9 +66,9 @@ def tile_mixerblock_pa_s_kernel(tc, x_proj, mix_mat, mix_b, out_w, out_b, out):
                 in_=mix_mat[:, j * P : (j + 1) * P, j * CHUNK :].rearrange("h p s -> p h s"),
             )
 
-        nc.vector.memset(bias_rows[:], 0.0)
-        nc.scalar.dma_start(out=bias_rows[: HEADS * N_CHUNKS, :], in_=mix_b.rearrange("h (i s) -> (h i) s", s=CHUNK))
-        nc.scalar.dma_start(
+        nc.gpsimd.memset(bias_rows[:], 0.0)
+        nc.sync.dma_start(out=bias_rows[: HEADS * N_CHUNKS, :], in_=mix_b.rearrange("h (i s) -> (h i) s", s=CHUNK))
+        nc.sync.dma_start(
             out=bias_rows[HEADS * N_CHUNKS : HEADS * N_CHUNKS + O_TILES, :], in_=out_b.rearrange("(m p) -> m p", p=P)
         )
         nc.sync.dma_start(out=x_raw[:], in_=x_proj.rearrange("b (j p) c -> p (b j) c", p=P))
@@ -97,9 +94,7 @@ def tile_mixerblock_pa_s_kernel(tc, x_proj, mix_mat, mix_b, out_w, out_b, out):
         nc.vector.tensor_copy(out=causal[:], in_=causal_f32[:])
 
         def regroup_x():
-            split = (HEADS - X_HEADS_ON_SCALAR) * P
-            nc.vector.tensor_copy(out=x_grouped[:, :split, :], in_=x_raw[:, :, :split].rearrange("p j c -> p c j"))
-            nc.scalar.copy(out=x_grouped[:, split:, :], in_=x_raw[:, :, split:].rearrange("p j c -> p c j"))
+            nc.vector.tensor_copy(out=x_grouped[:], in_=x_raw[:].rearrange("p j c -> p c j"))
 
         def quantise_x():
             nc.vector.quantize_mx(
@@ -109,21 +104,17 @@ def tile_mixerblock_pa_s_kernel(tc, x_proj, mix_mat, mix_b, out_w, out_b, out):
             )
 
         def stand_biases_up():
-            bias_cols = w_banks.tile([P, P], BF16, tag="w_t")
+            bias_cols = banks.tile([P, P], BF16, tag="spread")
             nc.tensor.transpose(bias_cols[:], bias_rows[:], ident[:])
             nc.vector.tensor_copy(out=mix_bias_cols[:], in_=bias_cols[:, : HEADS * N_CHUNKS])
             nc.vector.tensor_copy(out=out_bias[:], in_=bias_cols[:, HEADS * N_CHUNKS : HEADS * N_CHUNKS + O_TILES])
 
-        def spread_mix_bias():
-            for half in range(N_CHUNKS // 2):
-                spread = w_banks.tile([P, 2, HEADS, CHUNK], BF16, tag="w_t")
-                for k in range(2):
-                    for h in range(HEADS):
-                        r = h * N_CHUNKS + 2 * half + k
-                        nc.tensor.transpose(
-                            spread[:, k, h, :], mix_bias_cols[:, r : r + 1].to_broadcast([P, P]), ident[:]
-                        )
-                nc.scalar.copy(out=mix_bias[:, 2 * half : 2 * half + 2], in_=spread[:])
+        def spread_mix_bias(i):
+            spread = banks.tile([P, HEADS, CHUNK], BF16, tag="spread")
+            for h in range(HEADS):
+                r = h * N_CHUNKS + i
+                nc.tensor.transpose(spread[:, h, :], mix_bias_cols[:, r : r + 1].to_broadcast([P, P]), ident[:])
+            nc.scalar.copy(out=mix_bias[:, i], in_=spread[:])
 
         def mask_diagonal(i):
             nc.vector.tensor_tensor(
@@ -183,7 +174,7 @@ def tile_mixerblock_pa_s_kernel(tc, x_proj, mix_mat, mix_b, out_w, out_b, out):
 
         def transpose_out_w():
             for half in range(O_TILES // 2):
-                w_t = w_banks.tile([P, 2, PACK, P], BF16, tag="w_t")
+                w_t = banks.tile([P, 2, PACK, P], BF16)
                 for k in range(2):
                     for t in range(PACK):
                         nc.tensor.transpose(w_t[:, k, t, :], w_rows[:, 2 * half + k, t * P : (t + 1) * P], ident[:])
@@ -225,12 +216,12 @@ def tile_mixerblock_pa_s_kernel(tc, x_proj, mix_mat, mix_b, out_w, out_b, out):
                 in_=result[:, :, chunk_cols(i)],
             )
 
-        regroup_x()
         stand_biases_up()
+        spread_mix_bias(0)
+        regroup_x()
         mask_diagonal(0)
         quantise_x()
         regroup_mix(0)
-        spread_mix_bias()
         mask_diagonal(1)
         for step in range(N_CHUNKS + 2):
             if step < N_CHUNKS:
@@ -238,6 +229,7 @@ def tile_mixerblock_pa_s_kernel(tc, x_proj, mix_mat, mix_b, out_w, out_b, out):
                 mix_tokens(step)
             if step + 1 < N_CHUNKS:
                 regroup_mix(step + 1)
+                spread_mix_bias(step + 1)
             if step == 0:
                 transpose_out_w()
             if step >= 2:

@@ -17,14 +17,18 @@ CHANNELS = 512
 CHUNK = 128
 N_CHUNKS = TOKENS // CHUNK
 O_TILES = CHANNELS // P
+X_PARTS = 2
 MIX_HEADS_ON_SCALAR = 2
+RUN = 4
 
 FLOPS = 2 * HEADS * P * TOKENS * TOKENS + 2 * CHANNELS * CHANNELS * TOKENS
 
 
 def tile_mixerblock_pa_s_kernel(tc, x_proj, mix_mat, mix_b, out_w, out_b, out):
     nc = tc.nc
-    with tc.tile_pool(name="resident", bufs=1) as resident, tc.psum_pool(name="banks", bufs=2) as banks, tc.manual_schedule():
+    with tc.tile_pool(name="resident", bufs=1) as resident, tc.psum_pool(name="banks", bufs=2) as banks, tc.psum_pool(
+        name="out_banks", bufs=4
+    ) as out_banks, tc.manual_schedule():
         x_raw = resident.tile([P, PACK, CHANNELS], BF16)
         x_grouped = resident.tile([P, CHANNELS, PACK], BF16, align_bytes=64)
         x_codes = resident.tile([P, CHANNELS], U32, align_bytes=64)
@@ -60,6 +64,15 @@ def tile_mixerblock_pa_s_kernel(tc, x_proj, mix_mat, mix_b, out_w, out_b, out):
         def chunk_cols(i):
             return slice(i * CHUNK, (i + 1) * CHUNK)
 
+        def x_cols(part):
+            return slice(part * CHANNELS // X_PARTS, (part + 1) * CHANNELS // X_PARTS)
+
+        def regrouped(planes, words):
+            return dict(
+                out=words.rearrange("p (c r) j -> p c j r", r=RUN),
+                in_=planes.rearrange("p j (c r) -> p c j r", r=RUN),
+            )
+
         def load_mix_plane(j):
             nc.sync.dma_start(
                 out=mix_raw[:, j, :, j * CHUNK :],
@@ -71,11 +84,15 @@ def tile_mixerblock_pa_s_kernel(tc, x_proj, mix_mat, mix_b, out_w, out_b, out):
         nc.sync.dma_start(
             out=bias_rows[HEADS * N_CHUNKS : HEADS * N_CHUNKS + O_TILES, :], in_=out_b.rearrange("(m p) -> m p", p=P)
         )
-        nc.sync.dma_start(out=x_raw[:], in_=x_proj.rearrange("b (j p) c -> p (b j) c", p=P))
+        for part in range(X_PARTS):
+            nc.sync.dma_start(
+                out=x_raw[:, :, x_cols(part)],
+                in_=x_proj.rearrange("b (j p) c -> p (b j) c", p=P)[:, :, x_cols(part)],
+            )
         load_mix_plane(0)
         load_mix_plane(1)
-        nc.sync.dma_start(out=w_rows[:], in_=out_w.rearrange("(m p) c -> p m c", p=P))
         load_mix_plane(2)
+        nc.sync.dma_start(out=w_rows[:], in_=out_w.rearrange("(m p) c -> p m c", p=P))
         load_mix_plane(3)
 
         make_identity(nc, ident[:])
@@ -93,24 +110,24 @@ def tile_mixerblock_pa_s_kernel(tc, x_proj, mix_mat, mix_b, out_w, out_b, out):
             nc.vector.memset(mix_raw[:, j, :, : j * CHUNK], 0.0)
         nc.vector.tensor_copy(out=causal[:], in_=causal_f32[:])
 
-        def regroup_x():
-            nc.vector.tensor_copy(out=x_grouped[:], in_=x_raw[:].rearrange("p j c -> p c j"))
+        def regroup_x(part):
+            nc.vector.tensor_copy(**regrouped(x_raw[:, :, x_cols(part)], x_grouped[:, x_cols(part), :]))
 
-        def quantise_x():
+        def quantise_x(part):
             nc.vector.quantize_mx(
-                out=x_codes[:].bitcast(FP8X4),
-                scales=x_scales[:],
-                in_=x_grouped[:].rearrange("p c j -> p (c j)"),
+                out=x_codes[:, x_cols(part)].bitcast(FP8X4),
+                scales=x_scales[:, x_cols(part)],
+                in_=x_grouped[:, x_cols(part), :].rearrange("p c j -> p (c j)"),
             )
 
         def stand_biases_up():
-            bias_cols = banks.tile([P, P], BF16, tag="spread")
+            bias_cols = banks.tile([P, P], BF16, tag="transposed")
             nc.tensor.transpose(bias_cols[:], bias_rows[:], ident[:])
             nc.vector.tensor_copy(out=mix_bias_cols[:], in_=bias_cols[:, : HEADS * N_CHUNKS])
             nc.vector.tensor_copy(out=out_bias[:], in_=bias_cols[:, HEADS * N_CHUNKS : HEADS * N_CHUNKS + O_TILES])
 
         def spread_mix_bias(i):
-            spread = banks.tile([P, HEADS, CHUNK], BF16, tag="spread")
+            spread = banks.tile([P, HEADS, CHUNK], BF16, tag="transposed")
             for h in range(HEADS):
                 r = h * N_CHUNKS + i
                 nc.tensor.transpose(spread[:, h, :], mix_bias_cols[:, r : r + 1].to_broadcast([P, P]), ident[:])
@@ -125,15 +142,9 @@ def tile_mixerblock_pa_s_kernel(tc, x_proj, mix_mat, mix_b, out_w, out_b, out):
             )
 
         def regroup_mix(i):
-            split = HEADS - MIX_HEADS_ON_SCALAR
-            nc.vector.tensor_copy(
-                out=mix_grouped[:, i, :split],
-                in_=mix_raw[:, :, :split, chunk_cols(i)].rearrange("p j h s -> p h s j"),
-            )
-            nc.scalar.copy(
-                out=mix_grouped[:, i, split:],
-                in_=mix_raw[:, :, split:, chunk_cols(i)].rearrange("p j h s -> p h s j"),
-            )
+            for h in range(HEADS):
+                copy = nc.vector.tensor_copy if h < HEADS - MIX_HEADS_ON_SCALAR else nc.scalar.copy
+                copy(**regrouped(mix_raw[:, :, h, chunk_cols(i)], mix_grouped[:, i, h]))
 
         def quantise_mix(i):
             nc.vector.quantize_mx(
@@ -174,7 +185,7 @@ def tile_mixerblock_pa_s_kernel(tc, x_proj, mix_mat, mix_b, out_w, out_b, out):
 
         def transpose_out_w():
             for half in range(O_TILES // 2):
-                w_t = banks.tile([P, 2, PACK, P], BF16)
+                w_t = banks.tile([P, 2, PACK, P], BF16, tag="transposed")
                 for k in range(2):
                     for t in range(PACK):
                         nc.tensor.transpose(w_t[:, k, t, :], w_rows[:, 2 * half + k, t * P : (t + 1) * P], ident[:])
@@ -189,7 +200,7 @@ def tile_mixerblock_pa_s_kernel(tc, x_proj, mix_mat, mix_b, out_w, out_b, out):
             )
 
         def project(i):
-            projected = banks.tile([P, O_TILES, CHUNK], F32)
+            projected = out_banks.tile([P, O_TILES, CHUNK], F32)
             projected_banks[i] = projected
             for m in range(O_TILES):
                 rows = slice(m * P, (m + 1) * P)
@@ -204,12 +215,20 @@ def tile_mixerblock_pa_s_kernel(tc, x_proj, mix_mat, mix_b, out_w, out_b, out):
                 )
 
         def finish(i):
-            for m in range(O_TILES):
-                nc.scalar.activation(
-                    out=result[:, m, chunk_cols(i)],
-                    in_=projected_banks[i][:, m, :],
-                    func=ACT.Identity,
-                    bias=out_bias[:, m : m + 1],
+            if i < N_CHUNKS - 1:
+                for m in range(O_TILES):
+                    nc.scalar.activation(
+                        out=result[:, m, chunk_cols(i)],
+                        in_=projected_banks[i][:, m, :],
+                        func=ACT.Identity,
+                        bias=out_bias[:, m : m + 1],
+                    )
+            else:
+                nc.vector.tensor_tensor(
+                    out=result[:, :, chunk_cols(i)],
+                    in0=projected_banks[i][:],
+                    in1=out_bias[:].unsqueeze(2).to_broadcast([P, O_TILES, CHUNK]),
+                    op=ALU.add,
                 )
             nc.sync.dma_start(
                 out=out.rearrange("b (m p) s -> p (b m) s", p=P)[:, :, chunk_cols(i)],
@@ -218,28 +237,31 @@ def tile_mixerblock_pa_s_kernel(tc, x_proj, mix_mat, mix_b, out_w, out_b, out):
 
         stand_biases_up()
         spread_mix_bias(0)
-        regroup_x()
+        for part in range(X_PARTS):
+            regroup_x(part)
+        for part in range(X_PARTS):
+            quantise_x(part)
         mask_diagonal(0)
-        quantise_x()
         regroup_mix(0)
         mask_diagonal(1)
-        for step in range(N_CHUNKS + 2):
+        for step in range(N_CHUNKS + 3):
             if step < N_CHUNKS:
                 quantise_mix(step)
                 mix_tokens(step)
             if step + 1 < N_CHUNKS:
                 regroup_mix(step + 1)
                 spread_mix_bias(step + 1)
-            if step == 0:
+            if step == 1:
                 transpose_out_w()
-            if step >= 2:
-                finish(step - 2)
+            if step >= 3:
+                finish(step - 3)
             if 1 <= step <= N_CHUNKS:
                 add_mix_bias(step - 1)
-            if step == 1:
+            if step == 2:
                 quantise_out_w()
             if step + 2 < N_CHUNKS:
                 mask_diagonal(step + 2)
             if 1 <= step <= N_CHUNKS:
                 quantise_mixed(step - 1)
-                project(step - 1)
+            if 2 <= step <= N_CHUNKS + 1:
+                project(step - 2)

@@ -106,8 +106,8 @@ def tile_mixerblock_pa_s_kernel(tc, x_proj, mix_mat, mix_b, out_w, out_b, out):
             base=0,
             channel_multiplier=-1,
         )
-        for j in range(1, PACK):
-            nc.vector.memset(mix_raw[:, j, :, : j * CHUNK], 0.0)
+        for i in range(N_CHUNKS - 1):
+            nc.vector.memset(mix_grouped[:, i].rearrange("p h s j -> p (h s j)"), 0.0)
         nc.vector.tensor_copy(out=causal[:], in_=causal_f32[:])
 
         def regroup_x(part):
@@ -144,7 +144,7 @@ def tile_mixerblock_pa_s_kernel(tc, x_proj, mix_mat, mix_b, out_w, out_b, out):
         def regroup_mix(i):
             for h in range(HEADS):
                 copy = nc.vector.tensor_copy if h < HEADS - MIX_HEADS_ON_SCALAR else nc.scalar.copy
-                copy(**regrouped(mix_raw[:, :, h, chunk_cols(i)], mix_grouped[:, i, h]))
+                copy(**regrouped(mix_raw[:, : i + 1, h, chunk_cols(i)], mix_grouped[:, i, h, :, : i + 1]))
 
         def quantise_mix(i):
             nc.vector.quantize_mx(

@@ -17,6 +17,8 @@ CHANNELS = 512
 CHUNK = 128
 N_CHUNKS = TOKENS // CHUNK
 O_TILES = CHANNELS // P
+PAIR = 2 * CHUNK
+N_PAIRS = TOKENS // PAIR
 X_PARTS = 2
 MIX_HEADS_ON_SCALAR = 2
 RUN = 4
@@ -44,9 +46,11 @@ def tile_mixerblock_pa_s_kernel(tc, x_proj, mix_mat, mix_b, out_w, out_b, out):
         w_codes = resident.tile([P, CHANNELS], U32, align_bytes=64)
         w_scales = resident.tile([P, CHANNELS], U8, align_bytes=64)
 
-        bias_rows = resident.tile([P, P], BF16)
-        mix_bias_cols = resident.tile([P, HEADS * N_CHUNKS], BF16)
-        mix_bias = resident.tile([P, N_CHUNKS, HEADS, CHUNK], BF16)
+        mix_b_rows = resident.tile([P, P], F32)
+        mix_b_cols = resident.tile([P, HEADS * N_PAIRS], F32)
+        mix_b_wide = resident.tile([P, N_PAIRS, HEADS, P], F32)
+        mix_bias = resident.tile([P, N_PAIRS, HEADS, P], F32)
+        out_b_rows = resident.tile([P, P], BF16)
         out_bias = resident.tile([P, O_TILES], F32)
 
         y_grouped = resident.tile([P, N_CHUNKS, CHUNK, PACK], BF16, align_bytes=64)
@@ -55,10 +59,12 @@ def tile_mixerblock_pa_s_kernel(tc, x_proj, mix_mat, mix_b, out_w, out_b, out):
         result = resident.tile([P, O_TILES, TOKENS], F32)
 
         ident = resident.tile([P, P], BF16)
+        ident_f32 = resident.tile([P, P], F32)
         causal_f32 = resident.tile([P, P], F32)
         causal = resident.tile([P, P], BF16)
 
         mixed_banks = {}
+        spread_banks = {}
         projected_banks = {}
 
         def chunk_cols(i):
@@ -79,11 +85,12 @@ def tile_mixerblock_pa_s_kernel(tc, x_proj, mix_mat, mix_b, out_w, out_b, out):
                 in_=mix_mat[:, j * P : (j + 1) * P, j * CHUNK :].rearrange("h p s -> p h s"),
             )
 
-        nc.gpsimd.memset(bias_rows[:], 0.0)
-        nc.sync.dma_start(out=bias_rows[: HEADS * N_CHUNKS, :], in_=mix_b.rearrange("h (i s) -> (h i) s", s=CHUNK))
+        nc.gpsimd.memset(mix_b_rows[:], 0.0)
+        nc.gpsimd.memset(out_b_rows[:], 0.0)
         nc.sync.dma_start(
-            out=bias_rows[HEADS * N_CHUNKS : HEADS * N_CHUNKS + O_TILES, :], in_=out_b.rearrange("(m p) -> m p", p=P)
+            out=mix_b_rows[:].bitcast(BF16)[: HEADS * N_PAIRS, :], in_=mix_b.rearrange("h (q s) -> (h q) s", s=PAIR)
         )
+        nc.sync.dma_start(out=out_b_rows[:O_TILES, :], in_=out_b.rearrange("(m p) -> m p", p=P))
         for part in range(X_PARTS):
             nc.sync.dma_start(
                 out=x_raw[:, :, x_cols(part)],
@@ -95,6 +102,7 @@ def tile_mixerblock_pa_s_kernel(tc, x_proj, mix_mat, mix_b, out_w, out_b, out):
         nc.sync.dma_start(out=w_rows[:], in_=out_w.rearrange("(m p) c -> p m c", p=P))
         load_mix_plane(3)
 
+        make_identity(nc, ident_f32[:])
         make_identity(nc, ident[:])
         nc.gpsimd.memset(causal_f32[:], 1.0)
         nc.gpsimd.affine_select(
@@ -107,7 +115,7 @@ def tile_mixerblock_pa_s_kernel(tc, x_proj, mix_mat, mix_b, out_w, out_b, out):
             channel_multiplier=-1,
         )
         for i in range(N_CHUNKS - 1):
-            nc.vector.memset(mix_grouped[:, i].rearrange("p h s j -> p (h s j)"), 0.0)
+            nc.vector.memset(mix_grouped[:, i].rearrange("p h s j -> p (h s j)").bitcast(U32), 0)
         nc.vector.tensor_copy(out=causal[:], in_=causal_f32[:])
 
         def regroup_x(part):
@@ -121,17 +129,23 @@ def tile_mixerblock_pa_s_kernel(tc, x_proj, mix_mat, mix_b, out_w, out_b, out):
             )
 
         def stand_biases_up():
-            bias_cols = banks.tile([P, P], BF16, tag="transposed")
-            nc.tensor.transpose(bias_cols[:], bias_rows[:], ident[:])
-            nc.vector.tensor_copy(out=mix_bias_cols[:], in_=bias_cols[:, : HEADS * N_CHUNKS])
-            nc.vector.tensor_copy(out=out_bias[:], in_=bias_cols[:, HEADS * N_CHUNKS : HEADS * N_CHUNKS + O_TILES])
+            words = banks.tile([P, P], F32, tag="transposed")
+            nc.tensor.transpose(words[:], mix_b_rows[:], ident_f32[:])
+            nc.vector.tensor_copy(out=mix_b_cols[:], in_=words[:, : HEADS * N_PAIRS])
+            values = banks.tile([P, P], BF16, tag="transposed")
+            nc.tensor.transpose(values[:], out_b_rows[:], ident[:])
+            nc.vector.tensor_copy(out=out_bias[:], in_=values[:, :O_TILES])
 
-        def spread_mix_bias(i):
-            spread = banks.tile([P, HEADS, CHUNK], BF16, tag="transposed")
+        def spread_mix_bias(q):
+            cols = mix_b_cols[:].rearrange("p (h q) -> p q h", q=N_PAIRS)
+            nc.scalar.copy(out=mix_b_wide[:, q], in_=cols[:, q].unsqueeze(2).to_broadcast([P, HEADS, P]))
+            spread = banks.tile([P, HEADS, P], F32, tag="transposed")
+            spread_banks[q] = spread
             for h in range(HEADS):
-                r = h * N_CHUNKS + i
-                nc.tensor.transpose(spread[:, h, :], mix_bias_cols[:, r : r + 1].to_broadcast([P, P]), ident[:])
-            nc.scalar.copy(out=mix_bias[:, i], in_=spread[:])
+                nc.tensor.transpose(spread[:, h, :], mix_b_wide[:, q, h], ident_f32[:])
+
+        def copy_mix_bias(q):
+            nc.scalar.copy(out=mix_bias[:, q], in_=spread_banks[q][:])
 
         def mask_diagonal(i):
             nc.vector.tensor_tensor(
@@ -169,10 +183,11 @@ def tile_mixerblock_pa_s_kernel(tc, x_proj, mix_mat, mix_b, out_w, out_b, out):
                 )
 
         def add_mix_bias(i):
+            bias = mix_bias[:, i // 2].bitcast(BF16)[:, :, (i % 2) * CHUNK : (i % 2 + 1) * CHUNK]
             nc.vector.tensor_tensor(
                 out=y_grouped[:, i],
                 in0=mixed_banks[i][:].rearrange("p h s -> p s h"),
-                in1=mix_bias[:, i].rearrange("p h s -> p s h"),
+                in1=bias.rearrange("p h s -> p s h"),
                 op=ALU.add,
             )
 
@@ -236,13 +251,15 @@ def tile_mixerblock_pa_s_kernel(tc, x_proj, mix_mat, mix_b, out_w, out_b, out):
             )
 
         stand_biases_up()
-        spread_mix_bias(0)
+        for q in range(N_PAIRS):
+            spread_mix_bias(q)
         for part in range(X_PARTS):
             regroup_x(part)
         for part in range(X_PARTS):
             quantise_x(part)
         mask_diagonal(0)
         regroup_mix(0)
+        copy_mix_bias(0)
         mask_diagonal(1)
         for step in range(N_CHUNKS + 3):
             if step < N_CHUNKS:
@@ -250,7 +267,8 @@ def tile_mixerblock_pa_s_kernel(tc, x_proj, mix_mat, mix_b, out_w, out_b, out):
                 mix_tokens(step)
             if step + 1 < N_CHUNKS:
                 regroup_mix(step + 1)
-                spread_mix_bias(step + 1)
+            if step == 0:
+                copy_mix_bias(1)
             if step == 1:
                 transpose_out_w()
             if step >= 3:

@@ -20,7 +20,7 @@ O_TILES = CHANNELS // P
 PAIR = 2 * CHUNK
 N_PAIRS = TOKENS // PAIR
 X_PARTS = 2
-MIX_HEADS_ON_SCALAR = 2
+MIX_HEADS_ON_SCALAR = (2, 2, 2, 1)
 RUN = 4
 
 FLOPS = 2 * HEADS * P * TOKENS * TOKENS + 2 * CHANNELS * CHANNELS * TOKENS
@@ -50,8 +50,7 @@ def tile_mixerblock_pa_s_kernel(tc, x_proj, mix_mat, mix_b, out_w, out_b, out):
         mix_b_cols = resident.tile([P, HEADS * N_PAIRS], F32)
         mix_b_wide = resident.tile([P, N_PAIRS, HEADS, P], F32)
         mix_bias = resident.tile([P, N_PAIRS, HEADS, P], F32)
-        out_b_rows = resident.tile([P, P], BF16)
-        out_bias = resident.tile([P, O_TILES], F32)
+        out_bias = resident.tile([P, O_TILES], BF16)
 
         y_grouped = resident.tile([P, N_CHUNKS, CHUNK, PACK], BF16, align_bytes=64)
         y_codes = resident.tile([P, N_CHUNKS, CHUNK], U32, align_bytes=64)
@@ -86,24 +85,22 @@ def tile_mixerblock_pa_s_kernel(tc, x_proj, mix_mat, mix_b, out_w, out_b, out):
             )
 
         nc.gpsimd.memset(mix_b_rows[:], 0.0)
-        nc.gpsimd.memset(out_b_rows[:], 0.0)
-        nc.sync.dma_start(
-            out=mix_b_rows[:].bitcast(BF16)[: HEADS * N_PAIRS, :], in_=mix_b.rearrange("h (q s) -> (h q) s", s=PAIR)
-        )
-        nc.sync.dma_start(out=out_b_rows[:O_TILES, :], in_=out_b.rearrange("(m p) -> m p", p=P))
         for part in range(X_PARTS):
             nc.sync.dma_start(
                 out=x_raw[:, :, x_cols(part)],
                 in_=x_proj.rearrange("b (j p) c -> p (b j) c", p=P)[:, :, x_cols(part)],
             )
+        nc.sync.dma_start(
+            out=mix_b_rows[:].bitcast(BF16)[: HEADS * N_PAIRS, :], in_=mix_b.rearrange("h (q s) -> (h q) s", s=PAIR)
+        )
         load_mix_plane(0)
         load_mix_plane(1)
         load_mix_plane(2)
-        nc.sync.dma_start(out=w_rows[:], in_=out_w.rearrange("(m p) c -> p m c", p=P))
+        nc.sync.dma_start(out=w_rows[:], in_=out_w.rearrange("(p m) c -> p m c", m=O_TILES))
         load_mix_plane(3)
+        nc.sync.dma_start(out=out_bias[:], in_=out_b.rearrange("(p m) -> p m", m=O_TILES))
 
         make_identity(nc, ident_f32[:])
-        make_identity(nc, ident[:])
         nc.gpsimd.memset(causal_f32[:], 1.0)
         nc.gpsimd.affine_select(
             out=causal_f32[:],
@@ -114,9 +111,9 @@ def tile_mixerblock_pa_s_kernel(tc, x_proj, mix_mat, mix_b, out_w, out_b, out):
             base=0,
             channel_multiplier=-1,
         )
+        make_identity(nc, ident[:])
         for i in range(N_CHUNKS - 1):
             nc.vector.memset(mix_grouped[:, i].rearrange("p h s j -> p (h s j)").bitcast(U32), 0)
-        nc.vector.tensor_copy(out=causal[:], in_=causal_f32[:])
 
         def regroup_x(part):
             nc.vector.tensor_copy(**regrouped(x_raw[:, :, x_cols(part)], x_grouped[:, x_cols(part), :]))
@@ -128,13 +125,10 @@ def tile_mixerblock_pa_s_kernel(tc, x_proj, mix_mat, mix_b, out_w, out_b, out):
                 in_=x_grouped[:, x_cols(part), :].rearrange("p c j -> p (c j)"),
             )
 
-        def stand_biases_up():
+        def stand_mix_bias_up():
             words = banks.tile([P, P], F32, tag="transposed")
             nc.tensor.transpose(words[:], mix_b_rows[:], ident_f32[:])
             nc.vector.tensor_copy(out=mix_b_cols[:], in_=words[:, : HEADS * N_PAIRS])
-            values = banks.tile([P, P], BF16, tag="transposed")
-            nc.tensor.transpose(values[:], out_b_rows[:], ident[:])
-            nc.vector.tensor_copy(out=out_bias[:], in_=values[:, :O_TILES])
 
         def spread_mix_bias(q):
             cols = mix_b_cols[:].rearrange("p (h q) -> p q h", q=N_PAIRS)
@@ -157,7 +151,7 @@ def tile_mixerblock_pa_s_kernel(tc, x_proj, mix_mat, mix_b, out_w, out_b, out):
 
         def regroup_mix(i):
             for h in range(HEADS):
-                copy = nc.vector.tensor_copy if h < HEADS - MIX_HEADS_ON_SCALAR else nc.scalar.copy
+                copy = nc.vector.tensor_copy if h < HEADS - MIX_HEADS_ON_SCALAR[i] else nc.scalar.copy
                 copy(**regrouped(mix_raw[:, : i + 1, h, chunk_cols(i)], mix_grouped[:, i, h, :, : i + 1]))
 
         def quantise_mix(i):
@@ -246,15 +240,16 @@ def tile_mixerblock_pa_s_kernel(tc, x_proj, mix_mat, mix_b, out_w, out_b, out):
                     op=ALU.add,
                 )
             nc.sync.dma_start(
-                out=out.rearrange("b (m p) s -> p (b m) s", p=P)[:, :, chunk_cols(i)],
+                out=out.rearrange("b (p m) s -> p (b m) s", m=O_TILES)[:, :, chunk_cols(i)],
                 in_=result[:, :, chunk_cols(i)],
             )
 
-        stand_biases_up()
-        for q in range(N_PAIRS):
-            spread_mix_bias(q)
         for part in range(X_PARTS):
             regroup_x(part)
+        stand_mix_bias_up()
+        for q in range(N_PAIRS):
+            spread_mix_bias(q)
+        nc.vector.tensor_copy(out=causal[:], in_=causal_f32[:])
         for part in range(X_PARTS):
             quantise_x(part)
         mask_diagonal(0)

@@ -20,7 +20,7 @@ O_TILES = CHANNELS // P
 PAIR = 2 * CHUNK
 N_PAIRS = TOKENS // PAIR
 X_PARTS = 2
-MIX_HEADS_ON_SCALAR = (2, 2, 2, 1)
+MIX_HEADS_ON_SCALAR = (1, 2, 2, 1)
 RUN = 4
 
 FLOPS = 2 * HEADS * P * TOKENS * TOKENS + 2 * CHANNELS * CHANNELS * TOKENS
@@ -63,6 +63,7 @@ def tile_mixerblock_pa_s_kernel(tc, x_proj, mix_mat, mix_b, out_w, out_b, out):
         causal = resident.tile([P, P], BF16)
 
         mixed_banks = {}
+        w_banks = {}
         spread_banks = {}
         projected_banks = {}
 
@@ -85,18 +86,14 @@ def tile_mixerblock_pa_s_kernel(tc, x_proj, mix_mat, mix_b, out_w, out_b, out):
             )
 
         nc.gpsimd.memset(mix_b_rows[:], 0.0)
-        for part in range(X_PARTS):
-            nc.sync.dma_start(
-                out=x_raw[:, :, x_cols(part)],
-                in_=x_proj.rearrange("b (j p) c -> p (b j) c", p=P)[:, :, x_cols(part)],
-            )
+        nc.sync.dma_start(out=x_raw[:], in_=x_proj.rearrange("b (j p) c -> p (b j) c", p=P))
         nc.sync.dma_start(
             out=mix_b_rows[:].bitcast(BF16)[: HEADS * N_PAIRS, :], in_=mix_b.rearrange("h (q s) -> (h q) s", s=PAIR)
         )
         load_mix_plane(0)
         load_mix_plane(1)
-        load_mix_plane(2)
         nc.sync.dma_start(out=w_rows[:], in_=out_w.rearrange("(p m) c -> p m c", m=O_TILES))
+        load_mix_plane(2)
         load_mix_plane(3)
         nc.sync.dma_start(out=out_bias[:], in_=out_b.rearrange("(p m) -> p m", m=O_TILES))
 
@@ -116,7 +113,8 @@ def tile_mixerblock_pa_s_kernel(tc, x_proj, mix_mat, mix_b, out_w, out_b, out):
             nc.vector.memset(mix_grouped[:, i].rearrange("p h s j -> p (h s j)").bitcast(U32), 0)
 
         def regroup_x(part):
-            nc.vector.tensor_copy(**regrouped(x_raw[:, :, x_cols(part)], x_grouped[:, x_cols(part), :]))
+            copy = nc.vector.tensor_copy if part == 0 else nc.scalar.copy
+            copy(**regrouped(x_raw[:, :, x_cols(part)], x_grouped[:, x_cols(part), :]))
 
         def quantise_x(part):
             nc.vector.quantize_mx(
@@ -198,8 +196,12 @@ def tile_mixerblock_pa_s_kernel(tc, x_proj, mix_mat, mix_b, out_w, out_b, out):
                 for k in range(2):
                     for t in range(PACK):
                         nc.tensor.transpose(w_t[:, k, t, :], w_rows[:, 2 * half + k, t * P : (t + 1) * P], ident[:])
+                w_banks[half] = w_t
+
+        def copy_out_w():
+            for half in range(O_TILES // 2):
                 for k in range(2):
-                    nc.scalar.copy(out=w_grouped[:, 2 * half + k], in_=w_t[:, k].rearrange("p t o -> p o t"))
+                    nc.scalar.copy(out=w_grouped[:, 2 * half + k], in_=w_banks[half][:, k].rearrange("p t o -> p o t"))
 
         def quantise_out_w():
             nc.vector.quantize_mx(
@@ -209,12 +211,15 @@ def tile_mixerblock_pa_s_kernel(tc, x_proj, mix_mat, mix_b, out_w, out_b, out):
             )
 
         def project(i):
-            projected = out_banks.tile([P, O_TILES, CHUNK], F32)
-            projected_banks[i] = projected
+            per_bank = O_TILES if i < N_CHUNKS - 1 else O_TILES // 2
+            projected_banks[i] = []
             for m in range(O_TILES):
+                if m % per_bank == 0:
+                    projected = out_banks.tile([P, per_bank, CHUNK], F32, tag="projected")
+                    projected_banks[i].append(projected)
                 rows = slice(m * P, (m + 1) * P)
                 nc.tensor.matmul_mx(
-                    out=projected[:, m, :],
+                    out=projected_banks[i][-1][:, m % per_bank, :],
                     lhsT=w_codes[:, rows].bitcast(FP8X4),
                     lhsT_scale=w_scales[:, rows],
                     rhs=y_codes[:, i, :].bitcast(FP8X4),
@@ -224,25 +229,29 @@ def tile_mixerblock_pa_s_kernel(tc, x_proj, mix_mat, mix_b, out_w, out_b, out):
                 )
 
         def finish(i):
-            if i < N_CHUNKS - 1:
-                for m in range(O_TILES):
-                    nc.scalar.activation(
-                        out=result[:, m, chunk_cols(i)],
-                        in_=projected_banks[i][:, m, :],
-                        func=ACT.Identity,
-                        bias=out_bias[:, m : m + 1],
+            m0 = 0
+            for k, bank in enumerate(projected_banks[i]):
+                tiles = O_TILES // len(projected_banks[i])
+                if i == 1 or (i == N_CHUNKS - 1 and k == 0):
+                    nc.vector.tensor_tensor(
+                        out=result[:, m0 : m0 + tiles, chunk_cols(i)],
+                        in0=bank[:],
+                        in1=out_bias[:, m0 : m0 + tiles].unsqueeze(2).to_broadcast([P, tiles, CHUNK]),
+                        op=ALU.add,
                     )
-            else:
-                nc.vector.tensor_tensor(
-                    out=result[:, :, chunk_cols(i)],
-                    in0=projected_banks[i][:],
-                    in1=out_bias[:].unsqueeze(2).to_broadcast([P, O_TILES, CHUNK]),
-                    op=ALU.add,
+                else:
+                    for m in range(tiles):
+                        nc.scalar.activation(
+                            out=result[:, m0 + m, chunk_cols(i)],
+                            in_=bank[:, m, :],
+                            func=ACT.Identity,
+                            bias=out_bias[:, m0 + m : m0 + m + 1],
+                        )
+                nc.sync.dma_start(
+                    out=out.rearrange("b (p m) s -> p (b m) s", m=O_TILES)[:, m0 : m0 + tiles, chunk_cols(i)],
+                    in_=result[:, m0 : m0 + tiles, chunk_cols(i)],
                 )
-            nc.sync.dma_start(
-                out=out.rearrange("b (p m) s -> p (b m) s", m=O_TILES)[:, :, chunk_cols(i)],
-                in_=result[:, :, chunk_cols(i)],
-            )
+                m0 += tiles
 
         for part in range(X_PARTS):
             regroup_x(part)
@@ -256,25 +265,34 @@ def tile_mixerblock_pa_s_kernel(tc, x_proj, mix_mat, mix_b, out_w, out_b, out):
         regroup_mix(0)
         copy_mix_bias(0)
         mask_diagonal(1)
-        for step in range(N_CHUNKS + 3):
-            if step < N_CHUNKS:
-                quantise_mix(step)
-                mix_tokens(step)
-            if step + 1 < N_CHUNKS:
-                regroup_mix(step + 1)
+        for step in range(N_CHUNKS - 1):
+            quantise_mix(step)
+            mix_tokens(step)
+            regroup_mix(step + 1)
             if step == 0:
                 copy_mix_bias(1)
-            if step == 1:
                 transpose_out_w()
-            if step >= 3:
-                finish(step - 3)
-            if 1 <= step <= N_CHUNKS:
+            if step == 1:
+                copy_out_w()
+            if step >= 1:
                 add_mix_bias(step - 1)
             if step == 2:
                 quantise_out_w()
             if step + 2 < N_CHUNKS:
                 mask_diagonal(step + 2)
-            if 1 <= step <= N_CHUNKS:
+            if step >= 1:
                 quantise_mixed(step - 1)
-            if 2 <= step <= N_CHUNKS + 1:
-                project(step - 2)
+        project(0)
+        add_mix_bias(2)
+        project(1)
+        quantise_mix(3)
+        mix_tokens(3)
+        finish(0)
+        quantise_mixed(2)
+        project(2)
+        finish(1)
+        add_mix_bias(3)
+        finish(2)
+        quantise_mixed(3)
+        project(3)
+        finish(3)

@@ -20,7 +20,7 @@ O_TILES = CHANNELS // P
 PAIR = 2 * CHUNK
 N_PAIRS = TOKENS // PAIR
 X_PARTS = 2
-MIX_HEADS_ON_SCALAR = (1, 2, 2, 1)
+MIX_HEADS_ON_SCALAR = (1, 2, 2, 2)
 RUN = 4
 
 FLOPS = 2 * HEADS * P * TOKENS * TOKENS + 2 * CHANNELS * CHANNELS * TOKENS

import concourse.mybir as mybir
from concourse.masks import make_identity

BF16 = mybir.dt.bfloat16
F32 = mybir.dt.float32
U32 = mybir.dt.uint32
U8 = mybir.dt.uint8
FP8X4 = mybir.dt.float8_e4m3fn_x4
ALU = mybir.AluOpType
ACT = mybir.ActivationFunctionType

P = 128
PACK = 4
HEADS = 4
TOKENS = 512
CHANNELS = 512
CHUNK = 128
N_CHUNKS = TOKENS // CHUNK
O_TILES = CHANNELS // P
PAIR = 2 * CHUNK
N_PAIRS = TOKENS // PAIR
X_PARTS = 2
MIX_HEADS_ON_SCALAR = (1, 2, 2, 2)
RUN = 4

FLOPS = 2 * HEADS * P * TOKENS * TOKENS + 2 * CHANNELS * CHANNELS * TOKENS


def tile_mixerblock_pa_s_kernel(tc, x_proj, mix_mat, mix_b, out_w, out_b, out):
    nc = tc.nc
    with tc.tile_pool(name="resident", bufs=1) as resident, tc.psum_pool(name="banks", bufs=2) as banks, tc.psum_pool(
        name="out_banks", bufs=4
    ) as out_banks, tc.manual_schedule():
        x_raw = resident.tile([P, PACK, CHANNELS], BF16)
        x_grouped = resident.tile([P, CHANNELS, PACK], BF16, align_bytes=64)
        x_codes = resident.tile([P, CHANNELS], U32, align_bytes=64)
        x_scales = resident.tile([P, CHANNELS], U8, align_bytes=64)

        mix_raw = resident.tile([P, PACK, HEADS, TOKENS], BF16)
        mix_grouped = resident.tile([P, N_CHUNKS, HEADS, CHUNK, PACK], BF16, align_bytes=64)
        mix_codes = resident.tile([P, N_CHUNKS, HEADS * CHUNK], U32, align_bytes=64)
        mix_scales = resident.tile([P, N_CHUNKS, HEADS * CHUNK], U8, align_bytes=64)

        w_rows = resident.tile([P, O_TILES, CHANNELS], BF16)
        w_grouped = resident.tile([P, O_TILES, P, PACK], BF16, align_bytes=64)
        w_codes = resident.tile([P, CHANNELS], U32, align_bytes=64)
        w_scales = resident.tile([P, CHANNELS], U8, align_bytes=64)

        mix_b_rows = resident.tile([P, P], F32)
        mix_b_cols = resident.tile([P, HEADS * N_PAIRS], F32)
        mix_b_wide = resident.tile([P, N_PAIRS, HEADS, P], F32)
        mix_bias = resident.tile([P, N_PAIRS, HEADS, P], F32)
        out_bias = resident.tile([P, O_TILES], BF16)

        y_grouped = resident.tile([P, N_CHUNKS, CHUNK, PACK], BF16, align_bytes=64)
        y_codes = resident.tile([P, N_CHUNKS, CHUNK], U32, align_bytes=64)
        y_scales = resident.tile([P, N_CHUNKS, CHUNK], U8, align_bytes=64)
        result = resident.tile([P, O_TILES, TOKENS], F32)

        ident = resident.tile([P, P], BF16)
        ident_f32 = resident.tile([P, P], F32)
        causal_f32 = resident.tile([P, P], F32)
        causal = resident.tile([P, P], BF16)

        mixed_banks = {}
        w_banks = {}
        spread_banks = {}
        projected_banks = {}

        def chunk_cols(i):
            return slice(i * CHUNK, (i + 1) * CHUNK)

        def x_cols(part):
            return slice(part * CHANNELS // X_PARTS, (part + 1) * CHANNELS // X_PARTS)

        def regrouped(planes, words):
            return dict(
                out=words.rearrange("p (c r) j -> p c j r", r=RUN),
                in_=planes.rearrange("p j (c r) -> p c j r", r=RUN),
            )

        def load_mix_plane(j):
            nc.sync.dma_start(
                out=mix_raw[:, j, :, j * CHUNK :],
                in_=mix_mat[:, j * P : (j + 1) * P, j * CHUNK :].rearrange("h p s -> p h s"),
            )

        nc.gpsimd.memset(mix_b_rows[:], 0.0)
        nc.sync.dma_start(out=x_raw[:], in_=x_proj.rearrange("b (j p) c -> p (b j) c", p=P))
        nc.sync.dma_start(
            out=mix_b_rows[:].bitcast(BF16)[: HEADS * N_PAIRS, :], in_=mix_b.rearrange("h (q s) -> (h q) s", s=PAIR)
        )
        load_mix_plane(0)
        load_mix_plane(1)
        nc.sync.dma_start(out=w_rows[:], in_=out_w.rearrange("(p m) c -> p m c", m=O_TILES))
        load_mix_plane(2)
        load_mix_plane(3)
        nc.sync.dma_start(out=out_bias[:], in_=out_b.rearrange("(p m) -> p m", m=O_TILES))

        make_identity(nc, ident_f32[:])
        nc.gpsimd.memset(causal_f32[:], 1.0)
        nc.gpsimd.affine_select(
            out=causal_f32[:],
            in_=causal_f32[:],
            pattern=[[1, P]],
            compare_op=ALU.is_ge,
            fill=0.0,
            base=0,
            channel_multiplier=-1,
        )
        make_identity(nc, ident[:])
        for i in range(N_CHUNKS - 1):
            nc.vector.memset(mix_grouped[:, i].rearrange("p h s j -> p (h s j)").bitcast(U32), 0)

        def regroup_x(part):
            copy = nc.vector.tensor_copy if part == 0 else nc.scalar.copy
            copy(**regrouped(x_raw[:, :, x_cols(part)], x_grouped[:, x_cols(part), :]))

        def quantise_x(part):
            nc.vector.quantize_mx(
                out=x_codes[:, x_cols(part)].bitcast(FP8X4),
                scales=x_scales[:, x_cols(part)],
                in_=x_grouped[:, x_cols(part), :].rearrange("p c j -> p (c j)"),
            )

        def stand_mix_bias_up():
            words = banks.tile([P, P], F32, tag="transposed")
            nc.tensor.transpose(words[:], mix_b_rows[:], ident_f32[:])
            nc.vector.tensor_copy(out=mix_b_cols[:], in_=words[:, : HEADS * N_PAIRS])

        def spread_mix_bias(q):
            cols = mix_b_cols[:].rearrange("p (h q) -> p q h", q=N_PAIRS)
            nc.scalar.copy(out=mix_b_wide[:, q], in_=cols[:, q].unsqueeze(2).to_broadcast([P, HEADS, P]))
            spread = banks.tile([P, HEADS, P], F32, tag="transposed")
            spread_banks[q] = spread
            for h in range(HEADS):
                nc.tensor.transpose(spread[:, h, :], mix_b_wide[:, q, h], ident_f32[:])

        def copy_mix_bias(q):
            nc.scalar.copy(out=mix_bias[:, q], in_=spread_banks[q][:])

        def mask_diagonal(i):
            nc.vector.tensor_tensor(
                out=mix_raw[:, i, :, chunk_cols(i)],
                in0=mix_raw[:, i, :, chunk_cols(i)],
                in1=causal[:].unsqueeze(1).to_broadcast([P, HEADS, CHUNK]),
                op=ALU.mult,
            )

        def regroup_mix(i):
            for h in range(HEADS):
                copy = nc.vector.tensor_copy if h < HEADS - MIX_HEADS_ON_SCALAR[i] else nc.scalar.copy
                copy(**regrouped(mix_raw[:, : i + 1, h, chunk_cols(i)], mix_grouped[:, i, h, :, : i + 1]))

        def quantise_mix(i):
            nc.vector.quantize_mx(
                out=mix_codes[:, i, :].bitcast(FP8X4),
                scales=mix_scales[:, i, :],
                in_=mix_grouped[:, i].rearrange("p h s j -> p (h s j)"),
            )

        def mix_tokens(i):
            mixed = banks.tile([P, HEADS, CHUNK], F32)
            mixed_banks[i] = mixed
            for h in range(HEADS):
                head = slice(h * P, (h + 1) * P)
                nc.tensor.matmul_mx(
                    out=mixed[:, h, :],
                    lhsT=x_codes[:, head].bitcast(FP8X4),
                    lhsT_scale=x_scales[:, head],
                    rhs=mix_codes[:, i, head].bitcast(FP8X4),
                    rhs_scale=mix_scales[:, i, head],
                    start=True,
                    stop=True,
                )

        def add_mix_bias(i):
            bias = mix_bias[:, i // 2].bitcast(BF16)[:, :, (i % 2) * CHUNK : (i % 2 + 1) * CHUNK]
            nc.vector.tensor_tensor(
                out=y_grouped[:, i],
                in0=mixed_banks[i][:].rearrange("p h s -> p s h"),
                in1=bias.rearrange("p h s -> p s h"),
                op=ALU.add,
            )

        def quantise_mixed(i):
            nc.vector.quantize_mx(
                out=y_codes[:, i, :].bitcast(FP8X4),
                scales=y_scales[:, i, :],
                in_=y_grouped[:, i].rearrange("p s h -> p (s h)"),
            )

        def transpose_out_w():
            for half in range(O_TILES // 2):
                w_t = banks.tile([P, 2, PACK, P], BF16, tag="transposed")
                for k in range(2):
                    for t in range(PACK):
                        nc.tensor.transpose(w_t[:, k, t, :], w_rows[:, 2 * half + k, t * P : (t + 1) * P], ident[:])
                w_banks[half] = w_t

        def copy_out_w():
            for half in range(O_TILES // 2):
                for k in range(2):
                    nc.scalar.copy(out=w_grouped[:, 2 * half + k], in_=w_banks[half][:, k].rearrange("p t o -> p o t"))

        def quantise_out_w():
            nc.vector.quantize_mx(
                out=w_codes[:].bitcast(FP8X4),
                scales=w_scales[:],
                in_=w_grouped[:].rearrange("p m o t -> p (m o t)"),
            )

        def project(i):
            per_bank = O_TILES if i < N_CHUNKS - 1 else O_TILES // 2
            projected_banks[i] = []
            for m in range(O_TILES):
                if m % per_bank == 0:
                    projected = out_banks.tile([P, per_bank, CHUNK], F32, tag="projected")
                    projected_banks[i].append(projected)
                rows = slice(m * P, (m + 1) * P)
                nc.tensor.matmul_mx(
                    out=projected_banks[i][-1][:, m % per_bank, :],
                    lhsT=w_codes[:, rows].bitcast(FP8X4),
                    lhsT_scale=w_scales[:, rows],
                    rhs=y_codes[:, i, :].bitcast(FP8X4),
                    rhs_scale=y_scales[:, i, :],
                    start=True,
                    stop=True,
                )

        def finish(i):
            m0 = 0
            for k, bank in enumerate(projected_banks[i]):
                tiles = O_TILES // len(projected_banks[i])
                if i == 1 or (i == N_CHUNKS - 1 and k == 0):
                    nc.vector.tensor_tensor(
                        out=result[:, m0 : m0 + tiles, chunk_cols(i)],
                        in0=bank[:],
                        in1=out_bias[:, m0 : m0 + tiles].unsqueeze(2).to_broadcast([P, tiles, CHUNK]),
                        op=ALU.add,
                    )
                else:
                    for m in range(tiles):
                        nc.scalar.activation(
                            out=result[:, m0 + m, chunk_cols(i)],
                            in_=bank[:, m, :],
                            func=ACT.Identity,
                            bias=out_bias[:, m0 + m : m0 + m + 1],
                        )
                nc.sync.dma_start(
                    out=out.rearrange("b (p m) s -> p (b m) s", m=O_TILES)[:, m0 : m0 + tiles, chunk_cols(i)],
                    in_=result[:, m0 : m0 + tiles, chunk_cols(i)],
                )
                m0 += tiles

        for part in range(X_PARTS):
            regroup_x(part)
        stand_mix_bias_up()
        for q in range(N_PAIRS):
            spread_mix_bias(q)
        nc.vector.tensor_copy(out=causal[:], in_=causal_f32[:])
        for part in range(X_PARTS):
            quantise_x(part)
        mask_diagonal(0)
        regroup_mix(0)
        copy_mix_bias(0)
        mask_diagonal(1)
        for step in range(N_CHUNKS - 1):
            quantise_mix(step)
            mix_tokens(step)
            regroup_mix(step + 1)
            if step == 0:
                copy_mix_bias(1)
                transpose_out_w()
            if step == 1:
                copy_out_w()
            if step >= 1:
                add_mix_bias(step - 1)
            if step == 2:
                quantise_out_w()
            if step + 2 < N_CHUNKS:
                mask_diagonal(step + 2)
            if step >= 1:
                quantise_mixed(step - 1)
        project(0)
        add_mix_bias(2)
        project(1)
        quantise_mix(3)
        mix_tokens(3)
        finish(0)
        quantise_mixed(2)
        project(2)
        finish(1)
        add_mix_bias(3)
        finish(2)
        quantise_mixed(3)
        project(3)
        finish(3)
